import numpy as np
import ml_dtypes


def mxq(x, axis, fmt="e4m3"):
    dtype, down = {"e4m3": (ml_dtypes.float8_e4m3fn, 7), "e5m2": (ml_dtypes.float8_e5m2, 14)}[fmt]
    v = np.moveaxis(np.asarray(x, np.float32).astype(ml_dtypes.bfloat16).astype(np.float64), axis, -1)
    blocks = v.reshape(v.shape[:-1] + (-1, 32))
    amax = np.abs(blocks).max(-1, keepdims=True)
    byte = np.maximum(np.where(amax > 0, np.frexp(amax)[1] - 1 + 127, 0) - down, 1)
    scale = np.exp2(byte - 127.0)
    codes = (blocks / scale).astype(np.float32).astype(dtype).astype(np.float64)
    return np.moveaxis((codes * scale).reshape(v.shape), -1, axis)


WIDE = False


def mx_kscale(k):
    if not WIDE:
        return np.ones(k)
    levels = np.array([10, -10, 5, -5, 0])
    if k % 512:
        return np.exp2(np.random.permutation(np.resize(levels, k // 32))).repeat(32)
    a = np.empty((k // 512, 16))
    for p in range(k // 512):
        a[p, :8] = np.random.permutation(np.resize(levels, 8))
        for g in range(8):
            far = levels[np.abs(levels - a[p, g]) >= 10]
            a[p, g + 8] = far[np.random.randint(len(far))]
    return np.exp2(a.ravel()).repeat(32)


BF16 = ml_dtypes.bfloat16


def bf(x):
    return np.asarray(x, np.float32).astype(BF16)


def f64(x):
    return np.asarray(x).astype(np.float64)


B, T, C, F = 4, 128, 512, 16384
M = T


def silu(v):
    return v / (1.0 + np.exp(-v))


def sigmoid(v):
    return 1.0 / (1.0 + np.exp(-v))


def setup_inputs():
    t = mx_kscale(F)
    x = np.random.standard_normal((B, T, C)) + 0.5 * np.random.standard_normal((B, 1, C))
    return {"h": bf(silu(np.random.standard_normal((B, T, F)) * 0.85) * t),
            "x": bf(x),
            "memory": bf(np.random.standard_normal((1, M, C)) * 6.0 / np.sqrt(C)),
            "w2": bf(np.random.standard_normal((F, C)) * 3.0 / np.sqrt(F) / t[:, None]),
            "b2": bf(np.random.standard_normal(C) * 0.5)}


def reference(h, x, memory, w2, b2):
    update_gate = sigmoid((mxq(f64(h), 2, "e4m3") @ mxq(f64(w2), 0, "e4m3")) + f64(b2))
    x_mean = f64(x).mean(axis=1, keepdims=True)
    new_mem = f64(memory) * (1.0 - update_gate) + x_mean * update_gate
    return new_mem.mean(axis=0, keepdims=True)

@@ -1,0 +1,225 @@
+from contextlib import ExitStack
+
+import concourse.mybir as mybir
+from concourse.masks import make_identity
+
+BF16 = mybir.dt.bfloat16
+F32 = mybir.dt.float32
+U32 = mybir.dt.uint32
+U8 = mybir.dt.uint8
+FP8X4 = mybir.dt.float8_e4m3fn_x4
+SIGMOID = mybir.ActivationFunctionType.Sigmoid
+
+P = 128
+PACK = 4
+K_PASS = P * PACK
+
+BATCH, TOKENS, CHANNELS, HIDDEN = 4, 128, 512, 16384
+PASSES = HIDDEN // K_PASS
+
+CHUNK_PASSES = 4
+CHUNK = CHUNK_PASSES * K_PASS
+PAIR = 2
+RUNS_PER_CHUNK = BATCH // PAIR
+RUNS = (HIDDEN // CHUNK) * RUNS_PER_CHUNK
+WORDS_PER_BANK = 512
+PASSES_PER_BANK = 2
+
+STEP_PASSES = CHUNK_PASSES // RUNS_PER_CHUNK
+STEPS = PASSES // STEP_PASSES
+TRANSPOSE_LEAD = RUNS_PER_CHUNK + 1
+AHEAD = 3
+
+VECTOR_COLS = 320
+
+FLOPS = 2 * BATCH * TOKENS * HIDDEN * CHANNELS
+
+
+def tile_dynamicmemorybank_pb_k_kernel(tc, h, x, memory, w2, b2, out):
+    nc = tc.nc
+    with ExitStack() as ctx:
+        consts = ctx.enter_context(tc.tile_pool(name="consts", bufs=1))
+        h_raw_pool = ctx.enter_context(tc.tile_pool(name="h_raw", bufs=AHEAD * PAIR))
+        w_raw_pool = ctx.enter_context(tc.tile_pool(name="w_raw", bufs=AHEAD * STEP_PASSES))
+        grouped_pool = ctx.enter_context(tc.tile_pool(name="grouped", bufs=2 * STEP_PASSES))
+        h_mx_pool = ctx.enter_context(tc.tile_pool(name="h_mx", bufs=2 * RUNS_PER_CHUNK + 1))
+        w_mx_pool = ctx.enter_context(tc.tile_pool(name="w_mx", bufs=3 * STEP_PASSES))
+        blend_pool = ctx.enter_context(tc.tile_pool(name="blend", bufs=1))
+        acc_pool = ctx.enter_context(tc.psum_pool(name="acc", bufs=1))
+        bank_pool = ctx.enter_context(tc.psum_pool(name="bank", bufs=4))
+        ctx.enter_context(tc.manual_schedule())
+
+        h_raw = {}
+        w_raw = {}
+        h_grouped = {}
+        w_grouped = {}
+        h_mx = {}
+        w_mx = {}
+
+        def step_passes(step):
+            if 0 <= step < STEPS:
+                return range(step * STEP_PASSES, (step + 1) * STEP_PASSES)
+            return range(0)
+
+        def load_h(run):
+            chunk, pair = divmod(run, RUNS_PER_CHUNK)
+            for i in range(PAIR):
+                piece = h_raw_pool.tile([P, CHUNK], BF16, tag="h_raw")
+                nc.sync.dma_start(
+                    out=piece[:], in_=h[pair * PAIR + i, :, chunk * CHUNK : (chunk + 1) * CHUNK]
+                )
+                h_raw[(run, i)] = piece
+
+        def load_w(w_pass):
+            rows = w2[w_pass * K_PASS : (w_pass + 1) * K_PASS, :]
+            raw = w_raw_pool.tile([P, PACK, CHANNELS], BF16, tag="w_raw")
+            nc.sync.dma_start(out=raw[:], in_=rows.rearrange("(p t) c -> p t c", t=PACK))
+            w_raw[w_pass] = raw
+
+        def transpose_run(run):
+            banks = []
+            for i in range(PAIR):
+                words = h_raw[(run, i)][:].bitcast(F32)
+                for half in range(CHUNK_PASSES // PASSES_PER_BANK):
+                    bank = bank_pool.tile([P, WORDS_PER_BANK // P, P], F32, tag="bank")
+                    for slot in range(WORDS_PER_BANK // P):
+                        g, u = divmod(slot, 2)
+                        first = half * WORDS_PER_BANK + g * 2 * P
+                        nc.tensor.transpose(
+                            bank[:, slot, :], words[:, first + u : first + 2 * P : 2], identity[:]
+                        )
+                    banks.append(bank)
+            return banks
+
+        def copy_out_run(run, banks):
+            grouped = grouped_pool.tile([P, PAIR * CHUNK_PASSES * TOKENS * PACK], BF16, tag="h_grouped", align_bytes=64)
+            by_bank = grouped[:].bitcast(F32).rearrange(
+                "p (n g r u) -> p n g r u", n=len(banks), g=PASSES_PER_BANK, r=TOKENS, u=2
+            )
+            for n, bank in enumerate(banks):
+                nc.scalar.copy(
+                    out=by_bank[:, n],
+                    in_=bank[:].rearrange("p (g u) r -> p g r u", u=2),
+                )
+            h_grouped[run] = grouped
+
+        def quantise_h(run):
+            words = h_mx_pool.tile([P, PAIR * CHUNK_PASSES * TOKENS], U32, tag="h_words", align_bytes=64)
+            scales = h_mx_pool.tile([P, PAIR * CHUNK_PASSES * TOKENS], U8, tag="h_scales", align_bytes=64)
+            nc.vector.quantize_mx(out=words[:].bitcast(FP8X4), scales=scales[:], in_=h_grouped[run][:])
+            h_mx[run] = (words, scales)
+
+        def regroup_w(w_pass):
+            raw = w_raw[w_pass]
+            grouped = grouped_pool.tile([P, CHANNELS, PACK], BF16, tag="w_grouped", align_bytes=64)
+            nc.vector.tensor_copy(
+                out=grouped[:, :VECTOR_COLS, :].rearrange("p (c i) t -> p c t i", i=4),
+                in_=raw[:, :, :VECTOR_COLS].rearrange("p t (c i) -> p c t i", i=4),
+            )
+            nc.scalar.copy(
+                out=grouped[:, VECTOR_COLS:, :].rearrange("p (c i) t -> p c t i", i=4),
+                in_=raw[:, :, VECTOR_COLS:].rearrange("p t (c i) -> p c t i", i=4),
+            )
+            w_grouped[w_pass] = grouped
+
+        def quantise_w(w_pass):
+            words = w_mx_pool.tile([P, CHANNELS], U32, tag="w_words", align_bytes=64)
+            scales = w_mx_pool.tile([P, CHANNELS], U8, tag="w_scales", align_bytes=64)
+            nc.vector.quantize_mx(
+                out=words[:].bitcast(FP8X4),
+                scales=scales[:],
+                in_=w_grouped[w_pass][:].rearrange("p c t -> p (c t)"),
+            )
+            w_mx[w_pass] = (words, scales)
+
+        def multiply(w_pass):
+            chunk, g = divmod(w_pass, CHUNK_PASSES)
+            w_words, w_scales = w_mx[w_pass]
+            for b in range(BATCH):
+                pair, i = divmod(b, PAIR)
+                h_words, h_scales = h_mx[chunk * RUNS_PER_CHUNK + pair]
+                first = (i * CHUNK_PASSES + g) * TOKENS
+                nc.tensor.matmul_mx(
+                    out=acc[b][:],
+                    lhsT=h_words[:, first : first + TOKENS].bitcast(FP8X4),
+                    lhsT_scale=h_scales[:, first : first + TOKENS],
+                    rhs=w_words[:].bitcast(FP8X4),
+                    rhs_scale=w_scales[:],
+                    start=(w_pass == 0),
+                    stop=(w_pass == PASSES - 1),
+                )
+
+        identity = consts.tile([P, P], F32)
+        make_identity(nc, identity[:])
+        warm = consts.tile([P, 2], F32)
+        nc.vector.memset(warm[:], 0.0)
+        nc.scalar.activation(out=warm[:, 1:2], in_=warm[:, 0:1], func=SIGMOID)
+        ones = consts.tile([P, P], BF16)
+        nc.vector.memset(ones[:], 1.0)
+        mean_quarter = consts.tile([P, P], BF16)
+        nc.vector.memset(mean_quarter[:], 1.0 / (TOKENS * BATCH))
+        b2_rows = consts.tile([P, CHANNELS], BF16)
+        nc.vector.memset(b2_rows[:], 0.0)
+
+        acc = [acc_pool.tile([P, CHANNELS], F32, name="acc%d" % b) for b in range(BATCH)]
+
+        x_sb = consts.tile([P, BATCH, CHANNELS], BF16)
+        nc.sync.dma_start(out=x_sb[:], in_=x.rearrange("b t c -> t b c"))
+        mem_bf = consts.tile([P, CHANNELS], BF16)
+        nc.sync.dma_start(out=mem_bf[:], in_=memory[0])
+        nc.sync.dma_start(out=b2_rows[0:1, :], in_=b2.rearrange("(o c) -> o c", o=1))
+        for run in range(AHEAD):
+            load_h(run)
+        for w_pass in step_passes(0):
+            load_w(w_pass)
+
+        mem_f32 = blend_pool.tile([P, CHANNELS], F32)
+        nc.vector.tensor_copy(out=mem_f32[:], in_=mem_bf[:])
+        mem_quarter = blend_pool.tile([P, CHANNELS], F32)
+        nc.vector.tensor_scalar_mul(out=mem_quarter[:], in0=mem_bf[:], scalar1=1.0 / BATCH)
+        slope = []
+        for b in range(BATCH):
+            mean_bank = bank_pool.tile([P, CHANNELS], F32, tag="bank")
+            nc.tensor.matmul(mean_bank[:], lhsT=mean_quarter[:], rhs=x_sb[:, b, :], start=True, stop=True)
+            slope_b = blend_pool.tile([P, CHANNELS], F32, name="slope%d" % b)
+            nc.vector.tensor_sub(out=slope_b[:], in0=mean_bank[:], in1=mem_quarter[:])
+            slope.append(slope_b)
+        bias_bank = bank_pool.tile([P, CHANNELS], F32, tag="bank")
+        nc.tensor.matmul(bias_bank[:], lhsT=ones[:], rhs=b2_rows[:], start=True, stop=True)
+        bias = blend_pool.tile([P, CHANNELS], F32)
+        nc.scalar.copy(out=bias[:], in_=bias_bank[:])
+
+        for step in range(-TRANSPOSE_LEAD, STEPS):
+            run = step + TRANSPOSE_LEAD
+            if run < RUNS:
+                banks = transpose_run(run)
+                if run + AHEAD < RUNS:
+                    load_h(run + AHEAD)
+            for w_pass in step_passes(step):
+                quantise_w(w_pass)
+            for w_pass in step_passes(step):
+                multiply(w_pass)
+            for w_pass in step_passes(step + 1):
+                regroup_w(w_pass)
+            for w_pass in step_passes(step + 1 + AHEAD):
+                load_w(w_pass)
+            if run < RUNS:
+                copy_out_run(run, banks)
+            if 0 <= run - 1 < RUNS:
+                quantise_h(run - 1)
+
+        gates = []
+        for b in range(BATCH):
+            logit = blend_pool.tile([P, CHANNELS], F32, name="logit%d" % b)
+            nc.vector.tensor_add(out=logit[:], in0=acc[b][:], in1=bias[:])
+            gate = blend_pool.tile([P, CHANNELS], F32, name="gate%d" % b)
+            nc.scalar.activation(out=gate[:], in_=logit[:], func=SIGMOID)
+            gates.append(gate)
+        total = mem_f32
+        for b in range(BATCH):
+            term = blend_pool.tile([P, CHANNELS], F32, name="term%d" % b)
+            nc.vector.tensor_mul(out=term[:], in0=gates[b][:], in1=slope[b][:])
+            new_total = blend_pool.tile([P, CHANNELS], F32, name="total%d" % b)
+            nc.vector.tensor_add(out=new_total[:], in0=total[:], in1=term[:])
+            total = new_total
+        nc.sync.dma_start(out=out[0], in_=total[:])

@@ -132,22 +132,21 @@ def tile_dynamicmemorybank_pb_k_kernel(tc, h, x, memory, w2, b2, out):
             )
             w_mx[w_pass] = (words, scales)
 
-        def multiply(w_pass):
+        def multiply(w_pass, b):
             chunk, g = divmod(w_pass, CHUNK_PASSES)
             w_words, w_scales = w_mx[w_pass]
-            for b in range(BATCH):
-                pair, i = divmod(b, PAIR)
-                h_words, h_scales = h_mx[chunk * RUNS_PER_CHUNK + pair]
-                first = (i * CHUNK_PASSES + g) * TOKENS
-                nc.tensor.matmul_mx(
-                    out=acc[b][:],
-                    lhsT=h_words[:, first : first + TOKENS].bitcast(FP8X4),
-                    lhsT_scale=h_scales[:, first : first + TOKENS],
-                    rhs=w_words[:].bitcast(FP8X4),
-                    rhs_scale=w_scales[:],
-                    start=(w_pass == 0),
-                    stop=(w_pass == PASSES - 1),
-                )
+            pair, i = divmod(b, PAIR)
+            h_words, h_scales = h_mx[chunk * RUNS_PER_CHUNK + pair]
+            first = (i * CHUNK_PASSES + g) * TOKENS
+            nc.tensor.matmul_mx(
+                out=acc[b][:],
+                lhsT=h_words[:, first : first + TOKENS].bitcast(FP8X4),
+                lhsT_scale=h_scales[:, first : first + TOKENS],
+                rhs=w_words[:].bitcast(FP8X4),
+                rhs_scale=w_scales[:],
+                start=(w_pass == 0),
+                stop=(w_pass == PASSES - 1),
+            )
 
         identity = consts.tile([P, P], F32)
         make_identity(nc, identity[:])
@@ -197,8 +196,10 @@ def tile_dynamicmemorybank_pb_k_kernel(tc, h, x, memory, w2, b2, out):
                     load_h(run + AHEAD)
             for w_pass in step_passes(step):
                 quantise_w(w_pass)
-            for w_pass in step_passes(step):
-                multiply(w_pass)
+            if step < STEPS - 1:
+                for w_pass in step_passes(step):
+                    for b in range(BATCH):
+                        multiply(w_pass, b)
             for w_pass in step_passes(step + 1):
                 regroup_w(w_pass)
             for w_pass in step_passes(step + 1 + AHEAD):
@@ -208,18 +209,40 @@ def tile_dynamicmemorybank_pb_k_kernel(tc, h, x, memory, w2, b2, out):
             if 0 <= run - 1 < RUNS:
                 quantise_h(run - 1)
 
-        gates = []
+        logit = [blend_pool.tile([P, CHANNELS], F32, name="logit%d" % b) for b in range(BATCH)]
+        gate = [blend_pool.tile([P, CHANNELS], F32, name="gate%d" % b) for b in range(BATCH)]
+        term = [blend_pool.tile([P, CHANNELS], F32, name="term%d" % b) for b in range(BATCH)]
+        total = [blend_pool.tile([P, CHANNELS], F32, name="total%d" % b) for b in range(BATCH)]
+
+        def open_gate(b, cols):
+            nc.vector.tensor_add(out=logit[b][:, cols], in0=acc[b][:, cols], in1=bias[:, cols])
+            nc.scalar.activation(out=gate[b][:, cols], in_=logit[b][:, cols], func=SIGMOID)
+
+        def weigh(b, cols):
+            nc.vector.tensor_mul(out=term[b][:, cols], in0=gate[b][:, cols], in1=slope[b][:, cols])
+
+        def add_up(b, cols):
+            before = mem_f32 if b == 0 else total[b - 1]
+            nc.vector.tensor_add(out=total[b][:, cols], in0=before[:, cols], in1=term[b][:, cols])
+
+        every = slice(0, CHANNELS)
+        left, right = slice(0, CHANNELS // 2), slice(CHANNELS // 2, CHANNELS)
         for b in range(BATCH):
-            logit = blend_pool.tile([P, CHANNELS], F32, name="logit%d" % b)
-            nc.vector.tensor_add(out=logit[:], in0=acc[b][:], in1=bias[:])
-            gate = blend_pool.tile([P, CHANNELS], F32, name="gate%d" % b)
-            nc.scalar.activation(out=gate[:], in_=logit[:], func=SIGMOID)
-            gates.append(gate)
-        total = mem_f32
-        for b in range(BATCH):
-            term = blend_pool.tile([P, CHANNELS], F32, name="term%d" % b)
-            nc.vector.tensor_mul(out=term[:], in0=gates[b][:], in1=slope[b][:])
-            new_total = blend_pool.tile([P, CHANNELS], F32, name="total%d" % b)
-            nc.vector.tensor_add(out=new_total[:], in0=total[:], in1=term[:])
-            total = new_total
-        nc.sync.dma_start(out=out[0], in_=total[:])
+            for w_pass in step_passes(STEPS - 1):
+                multiply(w_pass, b)
+        open_gate(0, every)
+        open_gate(1, every)
+        weigh(0, every)
+        open_gate(2, every)
+        add_up(0, every)
+        weigh(1, every)
+        open_gate(3, left)
+        open_gate(3, right)
+        add_up(1, every)
+        weigh(2, every)
+        weigh(3, left)
+        add_up(2, every)
+        weigh(3, right)
+        for cols in (left, right):
+            add_up(3, cols)
+            nc.sync.dma_start(out=out[0][:, cols], in_=total[3][:, cols])

@@ -22,15 +22,19 @@ CHUNK = CHUNK_PASSES * K_PASS
 PAIR = 2
 RUNS_PER_CHUNK = BATCH // PAIR
 RUNS = (HIDDEN // CHUNK) * RUNS_PER_CHUNK
-WORDS_PER_BANK = 512
-PASSES_PER_BANK = 2
+BANK_PASSES = 2
+BANKS_PER_PIECE = CHUNK_PASSES // BANK_PASSES
 
 STEP_PASSES = CHUNK_PASSES // RUNS_PER_CHUNK
 STEPS = PASSES // STEP_PASSES
-TRANSPOSE_LEAD = RUNS_PER_CHUNK + 1
-AHEAD = 3
+TRANSPOSE_LEAD = 2
+LAST_RUN = RUNS - 1
+RAW_RUNS = 4
+RAW_STEPS = 4
 
-VECTOR_COLS = 320
+VECTOR_COLS = 304
+LATE_PASS = 26
+LATE_VECTOR_COLS = 256
 
 FLOPS = 2 * BATCH * TOKENS * HIDDEN * CHANNELS
 
@@ -39,10 +43,11 @@ def tile_dynamicmemorybank_pb_k_kernel(tc, h, x, memory, w2, b2, out):
     nc = tc.nc
     with ExitStack() as ctx:
         consts = ctx.enter_context(tc.tile_pool(name="consts", bufs=1))
-        h_raw_pool = ctx.enter_context(tc.tile_pool(name="h_raw", bufs=AHEAD * PAIR))
-        w_raw_pool = ctx.enter_context(tc.tile_pool(name="w_raw", bufs=AHEAD * STEP_PASSES))
-        grouped_pool = ctx.enter_context(tc.tile_pool(name="grouped", bufs=2 * STEP_PASSES))
-        h_mx_pool = ctx.enter_context(tc.tile_pool(name="h_mx", bufs=2 * RUNS_PER_CHUNK + 1))
+        h_raw_pool = ctx.enter_context(tc.tile_pool(name="h_raw", bufs=RAW_RUNS * PAIR))
+        w_raw_pool = ctx.enter_context(tc.tile_pool(name="w_raw", bufs=RAW_STEPS * STEP_PASSES))
+        h_grouped_pool = ctx.enter_context(tc.tile_pool(name="h_grouped", bufs=2 * PAIR))
+        w_grouped_pool = ctx.enter_context(tc.tile_pool(name="w_grouped", bufs=3 * STEP_PASSES))
+        h_mx_pool = ctx.enter_context(tc.tile_pool(name="h_mx", bufs=5 * PAIR))
         w_mx_pool = ctx.enter_context(tc.tile_pool(name="w_mx", bufs=3 * STEP_PASSES))
         blend_pool = ctx.enter_context(tc.tile_pool(name="blend", bufs=1))
         acc_pool = ctx.enter_context(tc.psum_pool(name="acc", bufs=1))
@@ -51,6 +56,7 @@ def tile_dynamicmemorybank_pb_k_kernel(tc, h, x, memory, w2, b2, out):
 
         h_raw = {}
         w_raw = {}
+        h_banks = {}
         h_grouped = {}
         w_grouped = {}
         h_mx = {}
@@ -70,55 +76,66 @@ def tile_dynamicmemorybank_pb_k_kernel(tc, h, x, memory, w2, b2, out):
                 )
                 h_raw[(run, i)] = piece
 
-        def load_w(w_pass):
-            rows = w2[w_pass * K_PASS : (w_pass + 1) * K_PASS, :]
-            raw = w_raw_pool.tile([P, PACK, CHANNELS], BF16, tag="w_raw")
-            nc.sync.dma_start(out=raw[:], in_=rows.rearrange("(p t) c -> p t c", t=PACK))
-            w_raw[w_pass] = raw
+        def load_w(step):
+            for w_pass in step_passes(step):
+                rows = w2[w_pass * K_PASS : (w_pass + 1) * K_PASS, :]
+                raw = w_raw_pool.tile([P, PACK, CHANNELS], BF16, tag="w_raw")
+                nc.sync.dma_start(out=raw[:], in_=rows.rearrange("(p t) c -> p t c", t=PACK))
+                w_raw[w_pass] = raw
 
-        def transpose_run(run):
+        to_load = [(load_h, 0)]
+        for run in range(1, LAST_RUN):
+            to_load += [(load_h, run), (load_w, run - 1)]
+        to_load += [(load_w, step) for step in range(LAST_RUN - 1, STEPS)] + [(load_h, LAST_RUN)]
+        free = {load_h: RAW_RUNS, load_w: RAW_STEPS}
+
+        def load_more():
+            while to_load and free[to_load[0][0]] > 0:
+                load, n = to_load[0]
+                to_load.remove(to_load[0])
+                free[load] -= 1
+                load(n)
+
+        def transpose_h(run, i):
+            words = h_raw[(run, i)][:].bitcast(F32)
             banks = []
-            for i in range(PAIR):
-                words = h_raw[(run, i)][:].bitcast(F32)
-                for half in range(CHUNK_PASSES // PASSES_PER_BANK):
-                    bank = bank_pool.tile([P, WORDS_PER_BANK // P, P], F32, tag="bank")
-                    for slot in range(WORDS_PER_BANK // P):
-                        g, u = divmod(slot, 2)
-                        first = half * WORDS_PER_BANK + g * 2 * P
+            for n in range(BANKS_PER_PIECE):
+                bank = bank_pool.tile([P, BANK_PASSES, 2, P], F32, tag="bank")
+                for g in range(BANK_PASSES):
+                    first = (n * BANK_PASSES + g) * 2 * P
+                    for u in range(2):
                         nc.tensor.transpose(
-                            bank[:, slot, :], words[:, first + u : first + 2 * P : 2], identity[:]
+                            bank[:, g, u, :], words[:, first + u : first + 2 * P : 2], identity[:]
                         )
-                    banks.append(bank)
-            return banks
+                banks.append(bank)
+            h_banks[(run, i)] = banks
 
-        def copy_out_run(run, banks):
-            grouped = grouped_pool.tile([P, PAIR * CHUNK_PASSES * TOKENS * PACK], BF16, tag="h_grouped", align_bytes=64)
+        def copy_out_h(run, i):
+            grouped = h_grouped_pool.tile([P, CHUNK_PASSES * TOKENS * PACK], BF16, tag="h_grouped", align_bytes=64)
             by_bank = grouped[:].bitcast(F32).rearrange(
-                "p (n g r u) -> p n g r u", n=len(banks), g=PASSES_PER_BANK, r=TOKENS, u=2
+                "p (n g r u) -> p n g r u", n=BANKS_PER_PIECE, g=BANK_PASSES, r=TOKENS, u=2
             )
-            for n, bank in enumerate(banks):
-                nc.scalar.copy(
-                    out=by_bank[:, n],
-                    in_=bank[:].rearrange("p (g u) r -> p g r u", u=2),
-                )
-            h_grouped[run] = grouped
+            for n, bank in enumerate(h_banks[(run, i)]):
+                nc.scalar.copy(out=by_bank[:, n], in_=bank[:].rearrange("p g u r -> p g r u"))
+            h_grouped[(run, i)] = grouped
 
-        def quantise_h(run):
-            words = h_mx_pool.tile([P, PAIR * CHUNK_PASSES * TOKENS], U32, tag="h_words", align_bytes=64)
-            scales = h_mx_pool.tile([P, PAIR * CHUNK_PASSES * TOKENS], U8, tag="h_scales", align_bytes=64)
-            nc.vector.quantize_mx(out=words[:].bitcast(FP8X4), scales=scales[:], in_=h_grouped[run][:])
-            h_mx[run] = (words, scales)
+        def quantise_h(run, i):
+            words = h_mx_pool.tile([P, CHUNK_PASSES * TOKENS], U32, tag="h_words", align_bytes=64)
+            scales = h_mx_pool.tile([P, CHUNK_PASSES * TOKENS], U8, tag="h_scales", align_bytes=64)
+            nc.vector.quantize_mx(out=words[:].bitcast(FP8X4), scales=scales[:], in_=h_grouped[(run, i)][:])
+            h_mx[(run, i)] = (words, scales)
 
         def regroup_w(w_pass):
             raw = w_raw[w_pass]
-            grouped = grouped_pool.tile([P, CHANNELS, PACK], BF16, tag="w_grouped", align_bytes=64)
+            split = VECTOR_COLS if w_pass < LATE_PASS else LATE_VECTOR_COLS
+            grouped = w_grouped_pool.tile([P, CHANNELS, PACK], BF16, tag="w_grouped", align_bytes=64)
             nc.vector.tensor_copy(
-                out=grouped[:, :VECTOR_COLS, :].rearrange("p (c i) t -> p c t i", i=4),
-                in_=raw[:, :, :VECTOR_COLS].rearrange("p t (c i) -> p c t i", i=4),
+                out=grouped[:, :split, :].rearrange("p (c i) t -> p c t i", i=4),
+                in_=raw[:, :, :split].rearrange("p t (c i) -> p c t i", i=4),
             )
             nc.scalar.copy(
-                out=grouped[:, VECTOR_COLS:, :].rearrange("p (c i) t -> p c t i", i=4),
-                in_=raw[:, :, VECTOR_COLS:].rearrange("p t (c i) -> p c t i", i=4),
+                out=grouped[:, split:, :].rearrange("p (c i) t -> p c t i", i=4),
+                in_=raw[:, :, split:].rearrange("p t (c i) -> p c t i", i=4),
             )
             w_grouped[w_pass] = grouped
 
@@ -134,14 +151,14 @@ def tile_dynamicmemorybank_pb_k_kernel(tc, h, x, memory, w2, b2, out):
 
         def multiply(w_pass, b):
             chunk, g = divmod(w_pass, CHUNK_PASSES)
-            w_words, w_scales = w_mx[w_pass]
             pair, i = divmod(b, PAIR)
-            h_words, h_scales = h_mx[chunk * RUNS_PER_CHUNK + pair]
-            first = (i * CHUNK_PASSES + g) * TOKENS
+            w_words, w_scales = w_mx[w_pass]
+            h_words, h_scales = h_mx[(chunk * RUNS_PER_CHUNK + pair, i)]
+            cols = slice(g * TOKENS, (g + 1) * TOKENS)
             nc.tensor.matmul_mx(
                 out=acc[b][:],
-                lhsT=h_words[:, first : first + TOKENS].bitcast(FP8X4),
-                lhsT_scale=h_scales[:, first : first + TOKENS],
+                lhsT=h_words[:, cols].bitcast(FP8X4),
+                lhsT_scale=h_scales[:, cols],
                 rhs=w_words[:].bitcast(FP8X4),
                 rhs_scale=w_scales[:],
                 start=(w_pass == 0),
@@ -167,13 +184,8 @@ def tile_dynamicmemorybank_pb_k_kernel(tc, h, x, memory, w2, b2, out):
         mem_bf = consts.tile([P, CHANNELS], BF16)
         nc.sync.dma_start(out=mem_bf[:], in_=memory[0])
         nc.sync.dma_start(out=b2_rows[0:1, :], in_=b2.rearrange("(o c) -> o c", o=1))
-        for run in range(AHEAD):
-            load_h(run)
-        for w_pass in step_passes(0):
-            load_w(w_pass)
+        load_more()
 
-        mem_f32 = blend_pool.tile([P, CHANNELS], F32)
-        nc.vector.tensor_copy(out=mem_f32[:], in_=mem_bf[:])
         mem_quarter = blend_pool.tile([P, CHANNELS], F32)
         nc.vector.tensor_scalar_mul(out=mem_quarter[:], in0=mem_bf[:], scalar1=1.0 / BATCH)
         slope = []
@@ -188,60 +200,80 @@ def tile_dynamicmemorybank_pb_k_kernel(tc, h, x, memory, w2, b2, out):
         bias = blend_pool.tile([P, CHANNELS], F32)
         nc.scalar.copy(out=bias[:], in_=bias_bank[:])
 
-        for step in range(-TRANSPOSE_LEAD, STEPS):
-            run = step + TRANSPOSE_LEAD
-            if run < RUNS:
-                banks = transpose_run(run)
-                if run + AHEAD < RUNS:
-                    load_h(run + AHEAD)
-            for w_pass in step_passes(step):
-                quantise_w(w_pass)
-            if step < STEPS - 1:
-                for w_pass in step_passes(step):
-                    for b in range(BATCH):
-                        multiply(w_pass, b)
-            for w_pass in step_passes(step + 1):
-                regroup_w(w_pass)
-            for w_pass in step_passes(step + 1 + AHEAD):
-                load_w(w_pass)
-            if run < RUNS:
-                copy_out_run(run, banks)
-            if 0 <= run - 1 < RUNS:
-                quantise_h(run - 1)
-
         logit = [blend_pool.tile([P, CHANNELS], F32, name="logit%d" % b) for b in range(BATCH)]
         gate = [blend_pool.tile([P, CHANNELS], F32, name="gate%d" % b) for b in range(BATCH)]
         term = [blend_pool.tile([P, CHANNELS], F32, name="term%d" % b) for b in range(BATCH)]
         total = [blend_pool.tile([P, CHANNELS], F32, name="total%d" % b) for b in range(BATCH)]
+        every = slice(0, CHANNELS)
+        left, right = slice(0, CHANNELS // 2), slice(CHANNELS // 2, CHANNELS)
 
-        def open_gate(b, cols):
+        def open_gate(b, cols=every):
             nc.vector.tensor_add(out=logit[b][:, cols], in0=acc[b][:, cols], in1=bias[:, cols])
             nc.scalar.activation(out=gate[b][:, cols], in_=logit[b][:, cols], func=SIGMOID)
 
-        def weigh(b, cols):
+        def weigh(b, cols=every):
             nc.vector.tensor_mul(out=term[b][:, cols], in0=gate[b][:, cols], in1=slope[b][:, cols])
 
-        def add_up(b, cols):
-            before = mem_f32 if b == 0 else total[b - 1]
+        def add_up(b, cols=every):
+            before = mem_bf if b == 0 else total[b - 1]
             nc.vector.tensor_add(out=total[b][:, cols], in0=before[:, cols], in1=term[b][:, cols])
 
-        every = slice(0, CHANNELS)
-        left, right = slice(0, CHANNELS // 2), slice(CHANNELS // 2, CHANNELS)
-        for b in range(BATCH):
-            for w_pass in step_passes(STEPS - 1):
+        for step in range(-TRANSPOSE_LEAD, LAST_RUN - 1):
+            run = step + TRANSPOSE_LEAD
+            if run < LAST_RUN:
+                for i in range(PAIR):
+                    transpose_h(run, i)
+                free[load_h] += 1
+                load_more()
+            if run > 0:
+                for i in range(PAIR):
+                    quantise_h(run - 1, i)
+            for w_pass in step_passes(step):
+                quantise_w(w_pass)
+            for w_pass in step_passes(step):
+                for b in range(BATCH):
+                    multiply(w_pass, b)
+            if run < LAST_RUN:
+                for i in range(PAIR):
+                    copy_out_h(run, i)
+            if step >= -1:
+                for w_pass in step_passes(step + 1):
+                    regroup_w(w_pass)
+                free[load_w] += 1
+                load_more()
+
+        def multiply_last(b):
+            for w_pass in range(PASSES - CHUNK_PASSES, PASSES):
                 multiply(w_pass, b)
-        open_gate(0, every)
-        open_gate(1, every)
-        weigh(0, every)
-        open_gate(2, every)
-        add_up(0, every)
-        weigh(1, every)
+
+        for w_pass in step_passes(STEPS - 2):
+            quantise_w(w_pass)
+        for w_pass in step_passes(STEPS - 1):
+            regroup_w(w_pass)
+        transpose_h(LAST_RUN, 0)
+        copy_out_h(LAST_RUN, 0)
+        for w_pass in step_passes(STEPS - 1):
+            quantise_w(w_pass)
+        multiply_last(0)
+        transpose_h(LAST_RUN, 1)
+        copy_out_h(LAST_RUN, 1)
+        quantise_h(LAST_RUN, 0)
+        multiply_last(1)
+        open_gate(0)
+        quantise_h(LAST_RUN, 1)
+        multiply_last(2)
+        open_gate(1)
+        weigh(0)
+        multiply_last(3)
+        open_gate(2)
+        add_up(0)
+        weigh(1)
         open_gate(3, left)
+        add_up(1)
         open_gate(3, right)
-        add_up(1, every)
-        weigh(2, every)
+        weigh(2)
         weigh(3, left)
-        add_up(2, every)
+        add_up(2)
         weigh(3, right)
         for cols in (left, right):
             add_up(3, cols)

@@ -33,8 +33,8 @@ RAW_RUNS = 4
 RAW_STEPS = 4
 
 VECTOR_COLS = 304
-LATE_PASS = 26
-LATE_VECTOR_COLS = 256
+LATE_PASS = 28
+LATE_VECTOR_COLS = 272
 
 FLOPS = 2 * BATCH * TOKENS * HIDDEN * CHANNELS
 
@@ -254,13 +254,13 @@ def tile_dynamicmemorybank_pb_k_kernel(tc, h, x, memory, w2, b2, out):
         copy_out_h(LAST_RUN, 0)
         for w_pass in step_passes(STEPS - 1):
             quantise_w(w_pass)
-        multiply_last(0)
         transpose_h(LAST_RUN, 1)
         copy_out_h(LAST_RUN, 1)
+        multiply_last(0)
         quantise_h(LAST_RUN, 0)
         multiply_last(1)
-        open_gate(0)
         quantise_h(LAST_RUN, 1)
+        open_gate(0)
         multiply_last(2)
         open_gate(1)
         weigh(0)

@@ -130,12 +130,12 @@ def tile_dynamicmemorybank_pb_k_kernel(tc, h, x, memory, w2, b2, out):
             split = VECTOR_COLS if w_pass < LATE_PASS else LATE_VECTOR_COLS
             grouped = w_grouped_pool.tile([P, CHANNELS, PACK], BF16, tag="w_grouped", align_bytes=64)
             nc.vector.tensor_copy(
-                out=grouped[:, :split, :].rearrange("p (c i) t -> p c t i", i=4),
-                in_=raw[:, :, :split].rearrange("p t (c i) -> p c t i", i=4),
+                out=grouped[:, :split, :].rearrange("p (c i) t -> p c t i", i=8),
+                in_=raw[:, :, :split].rearrange("p t (c i) -> p c t i", i=8),
             )
             nc.scalar.copy(
-                out=grouped[:, split:, :].rearrange("p (c i) t -> p c t i", i=4),
-                in_=raw[:, :, split:].rearrange("p t (c i) -> p c t i", i=4),
+                out=grouped[:, split:, :].rearrange("p (c i) t -> p c t i", i=8),
+                in_=raw[:, :, split:].rearrange("p t (c i) -> p c t i", i=8),
             )
             w_grouped[w_pass] = grouped
 

from contextlib import ExitStack

import concourse.mybir as mybir
from concourse.masks import make_identity

BF16 = mybir.dt.bfloat16
F32 = mybir.dt.float32
U32 = mybir.dt.uint32
U8 = mybir.dt.uint8
FP8X4 = mybir.dt.float8_e4m3fn_x4
SIGMOID = mybir.ActivationFunctionType.Sigmoid

P = 128
PACK = 4
K_PASS = P * PACK

BATCH, TOKENS, CHANNELS, HIDDEN = 4, 128, 512, 16384
PASSES = HIDDEN // K_PASS

CHUNK_PASSES = 4
CHUNK = CHUNK_PASSES * K_PASS
PAIR = 2
RUNS_PER_CHUNK = BATCH // PAIR
RUNS = (HIDDEN // CHUNK) * RUNS_PER_CHUNK
BANK_PASSES = 2
BANKS_PER_PIECE = CHUNK_PASSES // BANK_PASSES

STEP_PASSES = CHUNK_PASSES // RUNS_PER_CHUNK
STEPS = PASSES // STEP_PASSES
TRANSPOSE_LEAD = 2
LAST_RUN = RUNS - 1
RAW_RUNS = 4
RAW_STEPS = 4

VECTOR_COLS = 304
LATE_PASS = 28
LATE_VECTOR_COLS = 272

FLOPS = 2 * BATCH * TOKENS * HIDDEN * CHANNELS


def tile_dynamicmemorybank_pb_k_kernel(tc, h, x, memory, w2, b2, out):
    nc = tc.nc
    with ExitStack() as ctx:
        consts = ctx.enter_context(tc.tile_pool(name="consts", bufs=1))
        h_raw_pool = ctx.enter_context(tc.tile_pool(name="h_raw", bufs=RAW_RUNS * PAIR))
        w_raw_pool = ctx.enter_context(tc.tile_pool(name="w_raw", bufs=RAW_STEPS * STEP_PASSES))
        h_grouped_pool = ctx.enter_context(tc.tile_pool(name="h_grouped", bufs=2 * PAIR))
        w_grouped_pool = ctx.enter_context(tc.tile_pool(name="w_grouped", bufs=3 * STEP_PASSES))
        h_mx_pool = ctx.enter_context(tc.tile_pool(name="h_mx", bufs=5 * PAIR))
        w_mx_pool = ctx.enter_context(tc.tile_pool(name="w_mx", bufs=3 * STEP_PASSES))
        blend_pool = ctx.enter_context(tc.tile_pool(name="blend", bufs=1))
        acc_pool = ctx.enter_context(tc.psum_pool(name="acc", bufs=1))
        bank_pool = ctx.enter_context(tc.psum_pool(name="bank", bufs=4))
        ctx.enter_context(tc.manual_schedule())

        h_raw = {}
        w_raw = {}
        h_banks = {}
        h_grouped = {}
        w_grouped = {}
        h_mx = {}
        w_mx = {}

        def step_passes(step):
            if 0 <= step < STEPS:
                return range(step * STEP_PASSES, (step + 1) * STEP_PASSES)
            return range(0)

        def load_h(run):
            chunk, pair = divmod(run, RUNS_PER_CHUNK)
            for i in range(PAIR):
                piece = h_raw_pool.tile([P, CHUNK], BF16, tag="h_raw")
                nc.sync.dma_start(
                    out=piece[:], in_=h[pair * PAIR + i, :, chunk * CHUNK : (chunk + 1) * CHUNK]
                )
                h_raw[(run, i)] = piece

        def load_w(step):
            for w_pass in step_passes(step):
                rows = w2[w_pass * K_PASS : (w_pass + 1) * K_PASS, :]
                raw = w_raw_pool.tile([P, PACK, CHANNELS], BF16, tag="w_raw")
                nc.sync.dma_start(out=raw[:], in_=rows.rearrange("(p t) c -> p t c", t=PACK))
                w_raw[w_pass] = raw

        to_load = [(load_h, 0)]
        for run in range(1, LAST_RUN):
            to_load += [(load_h, run), (load_w, run - 1)]
        to_load += [(load_w, step) for step in range(LAST_RUN - 1, STEPS)] + [(load_h, LAST_RUN)]
        free = {load_h: RAW_RUNS, load_w: RAW_STEPS}

        def load_more():
            while to_load and free[to_load[0][0]] > 0:
                load, n = to_load[0]
                to_load.remove(to_load[0])
                free[load] -= 1
                load(n)

        def transpose_h(run, i):
            words = h_raw[(run, i)][:].bitcast(F32)
            banks = []
            for n in range(BANKS_PER_PIECE):
                bank = bank_pool.tile([P, BANK_PASSES, 2, P], F32, tag="bank")
                for g in range(BANK_PASSES):
                    first = (n * BANK_PASSES + g) * 2 * P
                    for u in range(2):
                        nc.tensor.transpose(
                            bank[:, g, u, :], words[:, first + u : first + 2 * P : 2], identity[:]
                        )
                banks.append(bank)
            h_banks[(run, i)] = banks

        def copy_out_h(run, i):
            grouped = h_grouped_pool.tile([P, CHUNK_PASSES * TOKENS * PACK], BF16, tag="h_grouped", align_bytes=64)
            by_bank = grouped[:].bitcast(F32).rearrange(
                "p (n g r u) -> p n g r u", n=BANKS_PER_PIECE, g=BANK_PASSES, r=TOKENS, u=2
            )
            for n, bank in enumerate(h_banks[(run, i)]):
                nc.scalar.copy(out=by_bank[:, n], in_=bank[:].rearrange("p g u r -> p g r u"))
            h_grouped[(run, i)] = grouped

        def quantise_h(run, i):
            words = h_mx_pool.tile([P, CHUNK_PASSES * TOKENS], U32, tag="h_words", align_bytes=64)
            scales = h_mx_pool.tile([P, CHUNK_PASSES * TOKENS], U8, tag="h_scales", align_bytes=64)
            nc.vector.quantize_mx(out=words[:].bitcast(FP8X4), scales=scales[:], in_=h_grouped[(run, i)][:])
            h_mx[(run, i)] = (words, scales)

        def regroup_w(w_pass):
            raw = w_raw[w_pass]
            split = VECTOR_COLS if w_pass < LATE_PASS else LATE_VECTOR_COLS
            grouped = w_grouped_pool.tile([P, CHANNELS, PACK], BF16, tag="w_grouped", align_bytes=64)
            nc.vector.tensor_copy(
                out=grouped[:, :split, :].rearrange("p (c i) t -> p c t i", i=8),
                in_=raw[:, :, :split].rearrange("p t (c i) -> p c t i", i=8),
            )
            nc.scalar.copy(
                out=grouped[:, split:, :].rearrange("p (c i) t -> p c t i", i=8),
                in_=raw[:, :, split:].rearrange("p t (c i) -> p c t i", i=8),
            )
            w_grouped[w_pass] = grouped

        def quantise_w(w_pass):
            words = w_mx_pool.tile([P, CHANNELS], U32, tag="w_words", align_bytes=64)
            scales = w_mx_pool.tile([P, CHANNELS], U8, tag="w_scales", align_bytes=64)
            nc.vector.quantize_mx(
                out=words[:].bitcast(FP8X4),
                scales=scales[:],
                in_=w_grouped[w_pass][:].rearrange("p c t -> p (c t)"),
            )
            w_mx[w_pass] = (words, scales)

        def multiply(w_pass, b):
            chunk, g = divmod(w_pass, CHUNK_PASSES)
            pair, i = divmod(b, PAIR)
            w_words, w_scales = w_mx[w_pass]
            h_words, h_scales = h_mx[(chunk * RUNS_PER_CHUNK + pair, i)]
            cols = slice(g * TOKENS, (g + 1) * TOKENS)
            nc.tensor.matmul_mx(
                out=acc[b][:],
                lhsT=h_words[:, cols].bitcast(FP8X4),
                lhsT_scale=h_scales[:, cols],
                rhs=w_words[:].bitcast(FP8X4),
                rhs_scale=w_scales[:],
                start=(w_pass == 0),
                stop=(w_pass == PASSES - 1),
            )

        identity = consts.tile([P, P], F32)
        make_identity(nc, identity[:])
        warm = consts.tile([P, 2], F32)
        nc.vector.memset(warm[:], 0.0)
        nc.scalar.activation(out=warm[:, 1:2], in_=warm[:, 0:1], func=SIGMOID)
        ones = consts.tile([P, P], BF16)
        nc.vector.memset(ones[:], 1.0)
        mean_quarter = consts.tile([P, P], BF16)
        nc.vector.memset(mean_quarter[:], 1.0 / (TOKENS * BATCH))
        b2_rows = consts.tile([P, CHANNELS], BF16)
        nc.vector.memset(b2_rows[:], 0.0)

        acc = [acc_pool.tile([P, CHANNELS], F32, name="acc%d" % b) for b in range(BATCH)]

        x_sb = consts.tile([P, BATCH, CHANNELS], BF16)
        nc.sync.dma_start(out=x_sb[:], in_=x.rearrange("b t c -> t b c"))
        mem_bf = consts.tile([P, CHANNELS], BF16)
        nc.sync.dma_start(out=mem_bf[:], in_=memory[0])
        nc.sync.dma_start(out=b2_rows[0:1, :], in_=b2.rearrange("(o c) -> o c", o=1))
        load_more()

        mem_quarter = blend_pool.tile([P, CHANNELS], F32)
        nc.vector.tensor_scalar_mul(out=mem_quarter[:], in0=mem_bf[:], scalar1=1.0 / BATCH)
        slope = []
        for b in range(BATCH):
            mean_bank = bank_pool.tile([P, CHANNELS], F32, tag="bank")
            nc.tensor.matmul(mean_bank[:], lhsT=mean_quarter[:], rhs=x_sb[:, b, :], start=True, stop=True)
            slope_b = blend_pool.tile([P, CHANNELS], F32, name="slope%d" % b)
            nc.vector.tensor_sub(out=slope_b[:], in0=mean_bank[:], in1=mem_quarter[:])
            slope.append(slope_b)
        bias_bank = bank_pool.tile([P, CHANNELS], F32, tag="bank")
        nc.tensor.matmul(bias_bank[:], lhsT=ones[:], rhs=b2_rows[:], start=True, stop=True)
        bias = blend_pool.tile([P, CHANNELS], F32)
        nc.scalar.copy(out=bias[:], in_=bias_bank[:])

        logit = [blend_pool.tile([P, CHANNELS], F32, name="logit%d" % b) for b in range(BATCH)]
        gate = [blend_pool.tile([P, CHANNELS], F32, name="gate%d" % b) for b in range(BATCH)]
        term = [blend_pool.tile([P, CHANNELS], F32, name="term%d" % b) for b in range(BATCH)]
        total = [blend_pool.tile([P, CHANNELS], F32, name="total%d" % b) for b in range(BATCH)]
        every = slice(0, CHANNELS)
        left, right = slice(0, CHANNELS // 2), slice(CHANNELS // 2, CHANNELS)

        def open_gate(b, cols=every):
            nc.vector.tensor_add(out=logit[b][:, cols], in0=acc[b][:, cols], in1=bias[:, cols])
            nc.scalar.activation(out=gate[b][:, cols], in_=logit[b][:, cols], func=SIGMOID)

        def weigh(b, cols=every):
            nc.vector.tensor_mul(out=term[b][:, cols], in0=gate[b][:, cols], in1=slope[b][:, cols])

        def add_up(b, cols=every):
            before = mem_bf if b == 0 else total[b - 1]
            nc.vector.tensor_add(out=total[b][:, cols], in0=before[:, cols], in1=term[b][:, cols])

        for step in range(-TRANSPOSE_LEAD, LAST_RUN - 1):
            run = step + TRANSPOSE_LEAD
            if run < LAST_RUN:
                for i in range(PAIR):
                    transpose_h(run, i)
                free[load_h] += 1
                load_more()
            if run > 0:
                for i in range(PAIR):
                    quantise_h(run - 1, i)
            for w_pass in step_passes(step):
                quantise_w(w_pass)
            for w_pass in step_passes(step):
                for b in range(BATCH):
                    multiply(w_pass, b)
            if run < LAST_RUN:
                for i in range(PAIR):
                    copy_out_h(run, i)
            if step >= -1:
                for w_pass in step_passes(step + 1):
                    regroup_w(w_pass)
                free[load_w] += 1
                load_more()

        def multiply_last(b):
            for w_pass in range(PASSES - CHUNK_PASSES, PASSES):
                multiply(w_pass, b)

        for w_pass in step_passes(STEPS - 2):
            quantise_w(w_pass)
        for w_pass in step_passes(STEPS - 1):
            regroup_w(w_pass)
        transpose_h(LAST_RUN, 0)
        copy_out_h(LAST_RUN, 0)
        for w_pass in step_passes(STEPS - 1):
            quantise_w(w_pass)
        transpose_h(LAST_RUN, 1)
        copy_out_h(LAST_RUN, 1)
        multiply_last(0)
        quantise_h(LAST_RUN, 0)
        multiply_last(1)
        quantise_h(LAST_RUN, 1)
        open_gate(0)
        multiply_last(2)
        open_gate(1)
        weigh(0)
        multiply_last(3)
        open_gate(2)
        add_up(0)
        weigh(1)
        open_gate(3, left)
        add_up(1)
        open_gate(3, right)
        weigh(2)
        weigh(3, left)
        add_up(2)
        weigh(3, right)
        for cols in (left, right):
            add_up(3, cols)
            nc.sync.dma_start(out=out[0][:, cols], in_=total[3][:, cols])
